import numpy as np
import ml_dtypes


def mxq(x, axis, fmt="e4m3"):
    dtype, down = {"e4m3": (ml_dtypes.float8_e4m3fn, 7), "e5m2": (ml_dtypes.float8_e5m2, 14)}[fmt]
    v = np.moveaxis(np.asarray(x, np.float32).astype(ml_dtypes.bfloat16).astype(np.float64), axis, -1)
    blocks = v.reshape(v.shape[:-1] + (-1, 32))
    amax = np.abs(blocks).max(-1, keepdims=True)
    byte = np.maximum(np.where(amax > 0, np.frexp(amax)[1] - 1 + 127, 0) - down, 1)
    scale = np.exp2(byte - 127.0)
    codes = (blocks / scale).astype(np.float32).astype(dtype).astype(np.float64)
    return np.moveaxis((codes * scale).reshape(v.shape), -1, axis)


WIDE = False


def mx_kscale(k):
    if not WIDE:
        return np.ones(k)
    levels = np.array([10, -10, 5, -5, 0])
    a = np.random.permutation(np.resize(levels, k // 512 * 4)).reshape(k // 512, 4)
    idx = np.arange(k)
    return np.exp2(a[idx // 512, idx % 128 // 32])


BF16 = ml_dtypes.bfloat16


def bf(x):
    return np.asarray(x, np.float32).astype(BF16)


def f64(x):
    return np.asarray(x).astype(np.float64)


E2M1 = np.array([0.0, 0.5, 1.0, 1.5, 2.0, 3.0, 4.0, 6.0, -0.0, -0.5, -1.0, -1.5, -2.0, -3.0, -4.0, -6.0])


def pack_weight(w, fmt):
    k, n = w.shape
    w = f64(bf(w)).reshape(k // 32, 32, n)
    amax = np.abs(w).max(1)
    if fmt == "e4m3":
        byte = np.frexp(amax)[1] - 1 + 127 - 7
    else:
        mant, ex = np.frexp(amax / 6.0)
        byte = np.where(mant > 0.5, ex, ex - 1) + 127
    byte = np.clip(np.where(amax > 0, byte, 1), 1, 254)
    scaled = (w * np.exp2(127.0 - byte)[:, None, :]).reshape(k, n).astype(np.float32)
    by_word = np.ascontiguousarray(scaled.reshape(k // 512, 128, 4, n).transpose(0, 1, 3, 2))
    if fmt == "e4m3":
        words = by_word.astype(ml_dtypes.float8_e4m3fn).view(np.uint8)
    else:
        c = by_word.astype(ml_dtypes.float4_e2m1fn).view(np.uint8) & 0xF
        words = c[..., 0::2] | (c[..., 1::2] << 4)
    return np.ascontiguousarray(words), np.ascontiguousarray(byte.astype(np.uint8).reshape(k // 512, 16, n))


def unpack_weight(words, scales, fmt):
    g, p, n, _ = words.shape
    if fmt == "e4m3":
        vals = np.ascontiguousarray(words).view(ml_dtypes.float8_e4m3fn).astype(np.float64)
    else:
        nib = np.empty((g, p, n, 4), np.uint8)
        nib[..., 0::2] = words & 0xF
        nib[..., 1::2] = words >> 4
        vals = E2M1[nib]
    vals = vals * np.repeat(np.exp2(scales.astype(np.float64) - 127.0), 8, axis=1)[..., None]
    return vals.transpose(0, 1, 3, 2).reshape(g * 512, n)

def pack4(w):
    words, scales = pack_weight(w, "e2m1")
    return words.reshape(words.shape[0], 128, -1), scales


def unpack4(words, scales):
    return unpack_weight(words.reshape(words.shape[0], 128, -1, 2), scales, "e2m1")


S, HID, H, KV, D, WINDOW, QB = 128, 8192, 8, 4, 256, 512, 512
NQ, NK = H * D, KV * D
EPS = 1e-6
ROPE_THETA = 10000.0


def rms_norm(x, w):
    var = np.mean(x * x, axis=-1, keepdims=True)
    return x * (1.0 / np.sqrt(var + EPS)) * (1.0 + w)


def rotate_half(x):
    x1, x2 = np.split(x, 2, axis=-1)
    return np.concatenate([-x2, x1], axis=-1)


def apply_rope(x, cos, sin):
    return x * cos[:, None, :] + rotate_half(x) * sin[:, None, :]


def setup_inputs():
    s = mx_kscale(HID)
    inv_freq = 1.0 / ROPE_THETA ** (np.arange(0, D, 2) / D)
    freqs = np.outer(np.arange(S), inv_freq)
    emb = np.concatenate([freqs, freqs], -1)
    hidden_states = bf(np.random.standard_normal((S, HID)) * s)
    words, scales = pack4(np.random.standard_normal((HID, NQ + NK + NK)) / np.sqrt(HID) / s[:, None])
    return {"hidden_states": hidden_states,
            "w_qkv_words": words, "w_qkv_scales": scales,
            "q_norm_w": bf(1.0 + 0.1 * np.random.standard_normal(D)),
            "k_norm_w": bf(1.0 + 0.1 * np.random.standard_normal(D)),
            "cos": bf(np.cos(emb)), "sin": bf(np.sin(emb))}


def reference(hidden_states, w_qkv_words, w_qkv_scales, q_norm_w, k_norm_w, cos, sin):
    qkv = mxq(f64(hidden_states), 1, "e4m3") @ unpack4(w_qkv_words, w_qkv_scales)
    q = qkv[:, :NQ].reshape(S, H, D)
    k = qkv[:, NQ:NQ + NK].reshape(S, KV, D)
    v = qkv[:, NQ + NK:].reshape(S, KV, D)
    q = rms_norm(q, f64(q_norm_w))
    k = rms_norm(k, f64(k_norm_w))
    q = apply_rope(q, f64(cos), f64(sin))
    k = apply_rope(k, f64(cos), f64(sin))
    return q, k, v

@@ -1,0 +1,230 @@
+from contextlib import ExitStack
+
+import concourse.mybir as mybir
+from concourse.masks import make_identity
+
+F32 = mybir.dt.float32
+BF16 = mybir.dt.bfloat16
+I32 = mybir.dt.int32
+U8 = mybir.dt.uint8
+U32 = mybir.dt.uint32
+FP8X4 = mybir.dt.float8_e4m3fn_x4
+FP4X4 = mybir.dt.float4_e2m1fn_x4
+ACT = mybir.ActivationFunctionType
+ALU = mybir.AluOpType
+
+P = 128
+TOKENS = 128
+HIDDEN = 8192
+K_PASS = 512
+PASSES = HIDDEN // K_PASS
+HEAD = 256
+HALF = HEAD // 2
+Q_HEADS, K_HEADS, V_HEADS = 8, 4, 4
+COLS = (Q_HEADS + K_HEADS + V_HEADS) * HEAD
+BANK_COLS = 512
+PSUM_BANKS = 8
+HEADS_PER_BANK = BANK_COLS // HEAD
+WORD_BYTES = 2
+EPS = 1e-6
+
+X_LOADS = 4
+PASSES_PER_BANK = 2
+PASSES_PER_QUANTISE = 4
+PLANES_PER_STEP = 4
+LOAD_BYTES = 8192
+WORD_BUFS = 8
+WORK_BUFS = 3
+
+FLOPS = 2 * TOKENS * HIDDEN * COLS
+
+
+def norm_and_rope(nc, work, acc, direct_table, crossed_table, out_rows):
+    raw = work.tile([P, HEADS_PER_BANK, 2, HALF], F32)
+    nc.scalar.copy(out=raw[:].rearrange("p h s d -> p (h s d)"), in_=acc[:])
+
+    squares = work.tile([P, HEADS_PER_BANK, HEAD], F32)
+    sumsq = work.tile([P, HEADS_PER_BANK], F32)
+    for h in range(HEADS_PER_BANK):
+        nc.scalar.activation(
+            out=squares[:, h, :],
+            in_=raw[:, h, :, :].rearrange("p s d -> p (s d)"),
+            func=ACT.Square,
+            accum_out=sumsq[:, h : h + 1],
+        )
+    mean_sq = work.tile([P, HEADS_PER_BANK], F32)
+    nc.vector.tensor_scalar(
+        out=mean_sq[:], in0=sumsq[:], scalar1=1.0 / HEAD, scalar2=EPS, op0=ALU.mult, op1=ALU.add
+    )
+    root = work.tile([P, HEADS_PER_BANK], F32)
+    nc.scalar.activation(out=root[:], in_=mean_sq[:], func=ACT.Sqrt)
+    rstd = work.tile([P, HEADS_PER_BANK], F32)
+    nc.vector.reciprocal(out=rstd[:], in_=root[:])
+
+    direct = work.tile([P, HEADS_PER_BANK, 2, HALF], F32)
+    nc.vector.tensor_tensor(
+        out=direct[:],
+        in0=raw[:],
+        in1=direct_table.unsqueeze(1).to_broadcast([P, HEADS_PER_BANK, 2, HALF]),
+        op=ALU.mult,
+    )
+    crossed = work.tile([P, HEADS_PER_BANK, 2, HALF], F32)
+    for s in range(2):
+        nc.vector.tensor_tensor(
+            out=crossed[:, :, s, :],
+            in0=raw[:, :, 1 - s, :],
+            in1=crossed_table[:, s, :].unsqueeze(1).to_broadcast([P, HEADS_PER_BANK, HALF]),
+            op=ALU.mult,
+        )
+    nc.vector.tensor_tensor(out=direct[:], in0=direct[:], in1=crossed[:], op=ALU.add)
+
+    rotated = work.tile([P, HEADS_PER_BANK, HEAD], F32)
+    for h in range(HEADS_PER_BANK):
+        nc.scalar.activation(
+            out=rotated[:, h, :],
+            in_=direct[:, h, :, :].rearrange("p s d -> p (s d)"),
+            func=ACT.Copy,
+            scale=rstd[:, h : h + 1],
+        )
+    nc.scalar.dma_start(out=out_rows, in_=rotated[:])
+
+
+def tile_gemmaattention_pa_k_kernel(
+    tc, hidden_states, w_qkv_words, w_qkv_scales, q_norm_w, k_norm_w, cos, sin, out_0, out_1, out_2
+):
+    nc = tc.nc
+    with ExitStack() as ctx:
+        keep = ctx.enter_context(tc.tile_pool(name="keep", bufs=1))
+        stream = ctx.enter_context(tc.tile_pool(name="stream", bufs=WORD_BUFS))
+        work = ctx.enter_context(tc.tile_pool(name="work", bufs=WORK_BUFS))
+        psum = ctx.enter_context(tc.psum_pool(name="psum", bufs=PSUM_BANKS))
+
+        x_sb = keep.tile([P, HIDDEN], BF16)
+        x_cols = HIDDEN // X_LOADS
+        for c in range(X_LOADS):
+            cols = slice(c * x_cols, (c + 1) * x_cols)
+            nc.sync.dma_start(out=x_sb[:, cols], in_=hidden_states[:, cols])
+        cos_sb = keep.tile([P, 2, HALF], BF16)
+        nc.scalar.dma_start(out=cos_sb[:], in_=cos.rearrange("r (s d) -> r s d", s=2))
+        sin_sb = keep.tile([P, 2, HALF], BF16)
+        nc.scalar.dma_start(out=sin_sb[:], in_=sin.rearrange("r (s d) -> r s d", s=2))
+
+        ones = keep.tile([P, P], BF16)
+        nc.vector.memset(ones[:], 1.0)
+        gain_rows = keep.tile([P, 2, HEAD], BF16)
+        nc.vector.memset(gain_rows[:], 0.0)
+        nc.scalar.dma_start(out=gain_rows[0:1, 0, :], in_=q_norm_w.rearrange("(o d) -> o d", o=1))
+        nc.scalar.dma_start(out=gain_rows[0:1, 1, :], in_=k_norm_w.rearrange("(o d) -> o d", o=1))
+        ident = keep.tile([P, P], F32)
+        make_identity(nc, ident[:])
+
+        planes = keep.tile([P, PASSES, COLS], U8, align_bytes=64)
+        for first in range(0, PASSES, PLANES_PER_STEP):
+            step = slice(first, first + PLANES_PER_STEP)
+            nc.vector.memset(planes[:, step, :].bitcast(I32), 0)
+        for first in range(0, PASSES, PLANES_PER_STEP):
+            step = slice(first, first + PLANES_PER_STEP)
+            for q in range(8):
+                part = 32 * (q // 4) + q % 4
+                nc.sync.dma_start(
+                    out=planes[part:P:64, step, :].bitcast(I32),
+                    in_=w_qkv_scales[step, q:16:8, :].bitcast(I32).rearrange("g q n -> q g n"),
+                )
+
+        gain_ps = psum.tile([P, BANK_COLS], F32, tag="bank")
+        nc.tensor.matmul(
+            out=gain_ps[:], lhsT=ones[:], rhs=gain_rows[:].rearrange("p w d -> p (w d)"), start=True, stop=True
+        )
+        gain = keep.tile([P, 2, 2, HALF], F32)
+        nc.vector.tensor_scalar_add(out=gain[:].rearrange("p w s d -> p (w s d)"), in0=gain_ps[:], scalar1=1.0)
+        sin_signed = keep.tile([P, 2, HALF], F32)
+        nc.vector.tensor_scalar_mul(out=sin_signed[:, 0, :], in0=sin_sb[:, 0, :], scalar1=-1.0)
+        nc.vector.tensor_copy(out=sin_signed[:, 1, :], in_=sin_sb[:, 1, :])
+        rope_direct = keep.tile([P, 2, 2, HALF], F32)
+        nc.vector.tensor_tensor(
+            out=rope_direct[:], in0=gain[:], in1=cos_sb[:].unsqueeze(1).to_broadcast([P, 2, 2, HALF]), op=ALU.mult
+        )
+        rope_crossed = keep.tile([P, 2, 2, HALF], F32)
+        for s in range(2):
+            nc.vector.tensor_tensor(
+                out=rope_crossed[:, :, s, :],
+                in0=gain[:, :, 1 - s, :],
+                in1=sin_signed[:, s, :].unsqueeze(1).to_broadcast([P, 2, HALF]),
+                op=ALU.mult,
+            )
+
+        x_words = x_sb[:].bitcast(F32)
+        grouped = keep.tile([P, PASSES * TOKENS * 4], BF16, align_bytes=64)
+        grouped_words = grouped[:].bitcast(F32).rearrange("p (g r u) -> p g r u", g=PASSES, u=2)
+        x_codes = keep.tile([P, PASSES * TOKENS], U32, align_bytes=64)
+        x_scales = keep.tile([P, PASSES * TOKENS], U8, align_bytes=64)
+        for j in range(PASSES // PASSES_PER_BANK):
+            xt = psum.tile([P, PASSES_PER_BANK, 2, TOKENS], F32, tag="bank")
+            for i in range(PASSES_PER_BANK):
+                g = j * PASSES_PER_BANK + i
+                for u in range(2):
+                    nc.tensor.transpose(xt[:, i, u, :], x_words[:, 256 * g + u : 256 * (g + 1) : 2], ident[:])
+            pair = slice(j * PASSES_PER_BANK, (j + 1) * PASSES_PER_BANK)
+            if j % 2 == 0:
+                nc.vector.tensor_copy(out=grouped_words[:, pair, :, :], in_=xt[:].rearrange("p g u r -> p g r u"))
+            else:
+                nc.scalar.copy(out=grouped_words[:, pair, :, :], in_=xt[:].rearrange("p g u r -> p g r u"))
+        for c in range(PASSES // PASSES_PER_QUANTISE):
+            width = PASSES_PER_QUANTISE * TOKENS
+            nc.vector.quantize_mx(
+                out=x_codes[:, c * width : (c + 1) * width].bitcast(FP8X4),
+                scales=x_scales[:, c * width : (c + 1) * width],
+                in_=grouped[:, 4 * c * width : 4 * (c + 1) * width],
+            )
+
+        blocks = (
+            (out_0, 0, Q_HEADS, 0),
+            (out_1, Q_HEADS * HEAD, K_HEADS, 1),
+            (out_2, (Q_HEADS + K_HEADS) * HEAD, V_HEADS, None),
+        )
+        for out_block, first_col, heads, table in blocks:
+            block_cols = heads * HEAD
+            banks = block_cols // BANK_COLS
+            passes_per_load = LOAD_BYTES // (WORD_BYTES * block_cols)
+            accs = [
+                psum.tile([P, BANK_COLS], F32, tag="bank", name="acc_%d_%d" % (first_col, b)) for b in range(banks)
+            ]
+            for first_pass in range(0, PASSES, passes_per_load):
+                words = stream.tile([P, LOAD_BYTES], U8, align_bytes=64)
+                nc.sync.dma_start(
+                    out=words[:].bitcast(I32).rearrange("p (g b) -> p g b", g=passes_per_load),
+                    in_=w_qkv_words[
+                        first_pass : first_pass + passes_per_load,
+                        :,
+                        WORD_BYTES * first_col : WORD_BYTES * (first_col + block_cols),
+                    ]
+                    .bitcast(I32)
+                    .rearrange("g p b -> p g b"),
+                )
+                for i in range(passes_per_load):
+                    g = first_pass + i
+                    for b in range(banks):
+                        byte0 = WORD_BYTES * (i * block_cols + b * BANK_COLS)
+                        col0 = first_col + b * BANK_COLS
+                        nc.tensor.matmul_mx(
+                            out=accs[b][:],
+                            lhsT=x_codes[:, g * TOKENS : (g + 1) * TOKENS].bitcast(FP8X4),
+                            lhsT_scale=x_scales[:, g * TOKENS : (g + 1) * TOKENS],
+                            rhs=words[:, byte0 : byte0 + WORD_BYTES * BANK_COLS].bitcast(FP4X4),
+                            rhs_scale=planes[:, g, col0 : col0 + BANK_COLS],
+                            start=(g == 0),
+                            stop=(g == PASSES - 1),
+                        )
+            for b in range(banks):
+                out_rows = out_block[:, b * HEADS_PER_BANK : (b + 1) * HEADS_PER_BANK, :]
+                if table is not None:
+                    norm_and_rope(nc, work, accs[b], rope_direct[:, table, :, :], rope_crossed[:, table, :, :], out_rows)
+                else:
+                    values = work.tile([P, HEADS_PER_BANK, HEAD], F32)
+                    flat = values[:].rearrange("p h d -> p (h d)")
+                    if b % 2 == 0:
+                        nc.scalar.copy(out=flat, in_=accs[b][:])
+                        nc.scalar.dma_start(out=out_rows, in_=values[:])
+                    else:
+                        nc.vector.tensor_copy(out=flat, in_=accs[b][:])
+                        nc.sync.dma_start(out=out_rows, in_=values[:])

@@ -31,62 +31,14 @@ EPS = 1e-6
 X_LOADS = 4
 PASSES_PER_BANK = 2
 PASSES_PER_QUANTISE = 4
-PLANES_PER_STEP = 4
+PLANE_COLS = 2048
+PLANE_PASSES = 8
+ZERO_PASSES = 4
 LOAD_BYTES = 8192
 WORD_BUFS = 8
 WORK_BUFS = 3
 
 FLOPS = 2 * TOKENS * HIDDEN * COLS
-
-
-def norm_and_rope(nc, work, acc, direct_table, crossed_table, out_rows):
-    raw = work.tile([P, HEADS_PER_BANK, 2, HALF], F32)
-    nc.scalar.copy(out=raw[:].rearrange("p h s d -> p (h s d)"), in_=acc[:])
-
-    squares = work.tile([P, HEADS_PER_BANK, HEAD], F32)
-    sumsq = work.tile([P, HEADS_PER_BANK], F32)
-    for h in range(HEADS_PER_BANK):
-        nc.scalar.activation(
-            out=squares[:, h, :],
-            in_=raw[:, h, :, :].rearrange("p s d -> p (s d)"),
-            func=ACT.Square,
-            accum_out=sumsq[:, h : h + 1],
-        )
-    mean_sq = work.tile([P, HEADS_PER_BANK], F32)
-    nc.vector.tensor_scalar(
-        out=mean_sq[:], in0=sumsq[:], scalar1=1.0 / HEAD, scalar2=EPS, op0=ALU.mult, op1=ALU.add
-    )
-    root = work.tile([P, HEADS_PER_BANK], F32)
-    nc.scalar.activation(out=root[:], in_=mean_sq[:], func=ACT.Sqrt)
-    rstd = work.tile([P, HEADS_PER_BANK], F32)
-    nc.vector.reciprocal(out=rstd[:], in_=root[:])
-
-    direct = work.tile([P, HEADS_PER_BANK, 2, HALF], F32)
-    nc.vector.tensor_tensor(
-        out=direct[:],
-        in0=raw[:],
-        in1=direct_table.unsqueeze(1).to_broadcast([P, HEADS_PER_BANK, 2, HALF]),
-        op=ALU.mult,
-    )
-    crossed = work.tile([P, HEADS_PER_BANK, 2, HALF], F32)
-    for s in range(2):
-        nc.vector.tensor_tensor(
-            out=crossed[:, :, s, :],
-            in0=raw[:, :, 1 - s, :],
-            in1=crossed_table[:, s, :].unsqueeze(1).to_broadcast([P, HEADS_PER_BANK, HALF]),
-            op=ALU.mult,
-        )
-    nc.vector.tensor_tensor(out=direct[:], in0=direct[:], in1=crossed[:], op=ALU.add)
-
-    rotated = work.tile([P, HEADS_PER_BANK, HEAD], F32)
-    for h in range(HEADS_PER_BANK):
-        nc.scalar.activation(
-            out=rotated[:, h, :],
-            in_=direct[:, h, :, :].rearrange("p s d -> p (s d)"),
-            func=ACT.Copy,
-            scale=rstd[:, h : h + 1],
-        )
-    nc.scalar.dma_start(out=out_rows, in_=rotated[:])
 
 
 def tile_gemmaattention_pa_k_kernel(
@@ -98,40 +50,83 @@ def tile_gemmaattention_pa_k_kernel(
         stream = ctx.enter_context(tc.tile_pool(name="stream", bufs=WORD_BUFS))
         work = ctx.enter_context(tc.tile_pool(name="work", bufs=WORK_BUFS))
         psum = ctx.enter_context(tc.psum_pool(name="psum", bufs=PSUM_BANKS))
+        ctx.enter_context(tc.manual_schedule())
 
         x_sb = keep.tile([P, HIDDEN], BF16)
         x_cols = HIDDEN // X_LOADS
         for c in range(X_LOADS):
             cols = slice(c * x_cols, (c + 1) * x_cols)
-            nc.sync.dma_start(out=x_sb[:, cols], in_=hidden_states[:, cols])
-        cos_sb = keep.tile([P, 2, HALF], BF16)
-        nc.scalar.dma_start(out=cos_sb[:], in_=cos.rearrange("r (s d) -> r s d", s=2))
-        sin_sb = keep.tile([P, 2, HALF], BF16)
-        nc.scalar.dma_start(out=sin_sb[:], in_=sin.rearrange("r (s d) -> r s d", s=2))
+            nc.scalar.dma_start(out=x_sb[:, cols], in_=hidden_states[:, cols])
 
-        ones = keep.tile([P, P], BF16)
-        nc.vector.memset(ones[:], 1.0)
-        gain_rows = keep.tile([P, 2, HEAD], BF16)
-        nc.vector.memset(gain_rows[:], 0.0)
-        nc.scalar.dma_start(out=gain_rows[0:1, 0, :], in_=q_norm_w.rearrange("(o d) -> o d", o=1))
-        nc.scalar.dma_start(out=gain_rows[0:1, 1, :], in_=k_norm_w.rearrange("(o d) -> o d", o=1))
         ident = keep.tile([P, P], F32)
         make_identity(nc, ident[:])
+        ones = keep.tile([P, P], BF16)
+        nc.gpsimd.memset(ones[:], 1.0)
+        gain_rows = keep.tile([P, 2, HEAD], BF16)
+        nc.gpsimd.memset(gain_rows[:], 0.0)
+        nc.gpsimd.dma_start(out=gain_rows[0:1, 0, :], in_=q_norm_w.rearrange("(o d) -> o d", o=1))
+        nc.gpsimd.dma_start(out=gain_rows[0:1, 1, :], in_=k_norm_w.rearrange("(o d) -> o d", o=1))
+        cos_sb = keep.tile([P, 2, HALF], BF16)
+        nc.gpsimd.dma_start(out=cos_sb[:], in_=cos.rearrange("r (s d) -> r s d", s=2))
+        sin_sb = keep.tile([P, 2, HALF], BF16)
+        nc.gpsimd.dma_start(out=sin_sb[:], in_=sin.rearrange("r (s d) -> r s d", s=2))
 
-        planes = keep.tile([P, PASSES, COLS], U8, align_bytes=64)
-        for first in range(0, PASSES, PLANES_PER_STEP):
-            step = slice(first, first + PLANES_PER_STEP)
-            nc.vector.memset(planes[:, step, :].bitcast(I32), 0)
-        for first in range(0, PASSES, PLANES_PER_STEP):
-            step = slice(first, first + PLANES_PER_STEP)
-            for q in range(8):
-                part = 32 * (q // 4) + q % 4
-                nc.sync.dma_start(
-                    out=planes[part:P:64, step, :].bitcast(I32),
-                    in_=w_qkv_scales[step, q:16:8, :].bitcast(I32).rearrange("g q n -> q g n"),
-                )
+        q_planes = keep.tile([P, PASSES, PLANE_COLS], U8, align_bytes=64)
+        kv_planes = keep.tile([P, PASSES, PLANE_COLS], U8, align_bytes=64)
 
-        gain_ps = psum.tile([P, BANK_COLS], F32, tag="bank")
+        def zero_planes(planes):
+            for first in range(0, PASSES, ZERO_PASSES):
+                nc.vector.memset(planes[:, first : first + ZERO_PASSES, :].bitcast(I32), 0)
+
+        def load_scale_rows(planes, first_col, first, r):
+            step = slice(first, first + PLANE_PASSES)
+            nc.sync.dma_start(
+                out=planes[r:P:32, step, :].bitcast(I32),
+                in_=w_qkv_scales[step, r:16:4, first_col : first_col + PLANE_COLS]
+                .bitcast(I32)
+                .rearrange("g q n -> q g n"),
+            )
+
+        zero_planes(q_planes)
+        for first in range(0, PASSES, PLANE_PASSES):
+            for r in range(4):
+                load_scale_rows(q_planes, 0, first, r)
+
+        x_words = x_sb[:].bitcast(F32)
+        grouped = keep.tile([P, PASSES * TOKENS * 4], BF16, align_bytes=64)
+        grouped_words = grouped[:].bitcast(F32).rearrange("p (g r u) -> p g r u", g=PASSES, u=2)
+        x_codes = keep.tile([P, PASSES * TOKENS], U32, align_bytes=64)
+        x_scales = keep.tile([P, PASSES * TOKENS], U8, align_bytes=64)
+
+        def transpose_bank(j):
+            xt = psum.tile([P, PASSES_PER_BANK, 2, TOKENS], F32, tag="bank", name="xt_%d" % j)
+            for i in range(PASSES_PER_BANK):
+                g = j * PASSES_PER_BANK + i
+                for u in range(2):
+                    nc.tensor.transpose(xt[:, i, u, :], x_words[:, 256 * g + u : 256 * (g + 1) : 2], ident[:])
+            pair = slice(j * PASSES_PER_BANK, (j + 1) * PASSES_PER_BANK)
+            if j % 2 == 0:
+                nc.vector.tensor_copy(out=grouped_words[:, pair, :, :], in_=xt[:].rearrange("p g u r -> p g r u"))
+            else:
+                nc.scalar.copy(out=grouped_words[:, pair, :, :], in_=xt[:].rearrange("p g u r -> p g r u"))
+
+        def quantise(c):
+            width = PASSES_PER_QUANTISE * TOKENS
+            nc.vector.quantize_mx(
+                out=x_codes[:, c * width : (c + 1) * width].bitcast(FP8X4),
+                scales=x_scales[:, c * width : (c + 1) * width],
+                in_=grouped[:, 4 * c * width : 4 * (c + 1) * width],
+            )
+
+        for c in range(PASSES // PASSES_PER_QUANTISE):
+            transpose_bank(2 * c)
+            transpose_bank(2 * c + 1)
+            if c > 0:
+                quantise(c - 1)
+        quantise(PASSES // PASSES_PER_QUANTISE - 1)
+        zero_planes(kv_planes)
+
+        gain_ps = psum.tile([P, BANK_COLS], F32, tag="bank", name="gain_ps")
         nc.tensor.matmul(
             out=gain_ps[:], lhsT=ones[:], rhs=gain_rows[:].rearrange("p w d -> p (w d)"), start=True, stop=True
         )
@@ -153,59 +148,90 @@ def tile_gemmaattention_pa_k_kernel(
                 op=ALU.mult,
             )
 
-        x_words = x_sb[:].bitcast(F32)
-        grouped = keep.tile([P, PASSES * TOKENS * 4], BF16, align_bytes=64)
-        grouped_words = grouped[:].bitcast(F32).rearrange("p (g r u) -> p g r u", g=PASSES, u=2)
-        x_codes = keep.tile([P, PASSES * TOKENS], U32, align_bytes=64)
-        x_scales = keep.tile([P, PASSES * TOKENS], U8, align_bytes=64)
-        for j in range(PASSES // PASSES_PER_BANK):
-            xt = psum.tile([P, PASSES_PER_BANK, 2, TOKENS], F32, tag="bank")
-            for i in range(PASSES_PER_BANK):
-                g = j * PASSES_PER_BANK + i
-                for u in range(2):
-                    nc.tensor.transpose(xt[:, i, u, :], x_words[:, 256 * g + u : 256 * (g + 1) : 2], ident[:])
-            pair = slice(j * PASSES_PER_BANK, (j + 1) * PASSES_PER_BANK)
-            if j % 2 == 0:
-                nc.vector.tensor_copy(out=grouped_words[:, pair, :, :], in_=xt[:].rearrange("p g u r -> p g r u"))
-            else:
-                nc.scalar.copy(out=grouped_words[:, pair, :, :], in_=xt[:].rearrange("p g u r -> p g r u"))
-        for c in range(PASSES // PASSES_PER_QUANTISE):
-            width = PASSES_PER_QUANTISE * TOKENS
-            nc.vector.quantize_mx(
-                out=x_codes[:, c * width : (c + 1) * width].bitcast(FP8X4),
-                scales=x_scales[:, c * width : (c + 1) * width],
-                in_=grouped[:, 4 * c * width : 4 * (c + 1) * width],
+        def square_and_rotate(acc, table):
+            by_half = acc[:].rearrange("p (h s d) -> p h s d", h=HEADS_PER_BANK, s=2)
+            squares = work.tile([P, HEAD], F32, name="squares")
+            sumsq = work.tile([P, HEADS_PER_BANK], F32, name="sumsq")
+            for h in range(HEADS_PER_BANK):
+                nc.scalar.activation(
+                    out=squares[:],
+                    in_=acc[:, h * HEAD : (h + 1) * HEAD],
+                    func=ACT.Square,
+                    accum_out=sumsq[:, h : h + 1],
+                )
+            direct = work.tile([P, HEADS_PER_BANK, 2, HALF], F32, name="direct")
+            nc.vector.tensor_tensor(
+                out=direct[:],
+                in0=by_half,
+                in1=rope_direct[:, table, :, :].unsqueeze(1).to_broadcast([P, HEADS_PER_BANK, 2, HALF]),
+                op=ALU.mult,
             )
+            crossed = work.tile([P, HEADS_PER_BANK, 2, HALF], F32, name="crossed")
+            for s in range(2):
+                nc.vector.tensor_tensor(
+                    out=crossed[:, :, s, :],
+                    in0=by_half[:, :, 1 - s, :],
+                    in1=rope_crossed[:, table, s, :].unsqueeze(1).to_broadcast([P, HEADS_PER_BANK, HALF]),
+                    op=ALU.mult,
+                )
+            mean_sq = work.tile([P, HEADS_PER_BANK], F32, name="mean_sq")
+            nc.vector.tensor_scalar(
+                out=mean_sq[:], in0=sumsq[:], scalar1=1.0 / HEAD, scalar2=EPS, op0=ALU.mult, op1=ALU.add
+            )
+            return direct, crossed, mean_sq
+
+        def scale_and_store(direct, crossed, mean_sq, out_rows):
+            root = work.tile([P, HEADS_PER_BANK], F32, name="root")
+            nc.scalar.activation(out=root[:], in_=mean_sq[:], func=ACT.Sqrt)
+            nc.vector.tensor_tensor(out=direct[:], in0=direct[:], in1=crossed[:], op=ALU.add)
+            rstd = work.tile([P, HEADS_PER_BANK], F32, name="rstd")
+            nc.vector.reciprocal(out=rstd[:], in_=root[:])
+            rotated = work.tile([P, HEADS_PER_BANK, HEAD], F32, name="rotated")
+            for h in range(HEADS_PER_BANK):
+                nc.scalar.activation(
+                    out=rotated[:, h, :],
+                    in_=direct[:, h, :, :].rearrange("p s d -> p (s d)"),
+                    func=ACT.Copy,
+                    scale=rstd[:, h : h + 1],
+                )
+            nc.scalar.dma_start(out=out_rows, in_=rotated[:])
 
         blocks = (
-            (out_0, 0, Q_HEADS, 0),
-            (out_1, Q_HEADS * HEAD, K_HEADS, 1),
-            (out_2, (Q_HEADS + K_HEADS) * HEAD, V_HEADS, None),
+            (out_0, 0, Q_HEADS, 0, (2,) * 8),
+            (out_1, Q_HEADS * HEAD, K_HEADS, 1, (4,) * 4),
+            (out_2, (Q_HEADS + K_HEADS) * HEAD, V_HEADS, None, (4, 4, 4, 2, 1, 1)),
         )
-        for out_block, first_col, heads, table in blocks:
+        kv_rows = [(first, r) for first in range(0, PASSES, PLANE_PASSES) for r in range(4)]
+        for out_block, first_col, heads, table, loads in blocks:
             block_cols = heads * HEAD
             banks = block_cols // BANK_COLS
-            passes_per_load = LOAD_BYTES // (WORD_BYTES * block_cols)
+            planes = q_planes if first_col < PLANE_COLS else kv_planes
             accs = [
                 psum.tile([P, BANK_COLS], F32, tag="bank", name="acc_%d_%d" % (first_col, b)) for b in range(banks)
             ]
-            for first_pass in range(0, PASSES, passes_per_load):
-                words = stream.tile([P, LOAD_BYTES], U8, align_bytes=64)
+            first_pass = 0
+            for n, load_passes in enumerate(loads):
+                load_bytes = load_passes * WORD_BYTES * block_cols
+                words = stream.tile([P, LOAD_BYTES], U8, align_bytes=64, name="words")
                 nc.sync.dma_start(
-                    out=words[:].bitcast(I32).rearrange("p (g b) -> p g b", g=passes_per_load),
+                    out=words[:, :load_bytes].bitcast(I32).rearrange("p (g b) -> p g b", g=load_passes),
                     in_=w_qkv_words[
-                        first_pass : first_pass + passes_per_load,
+                        first_pass : first_pass + load_passes,
                         :,
                         WORD_BYTES * first_col : WORD_BYTES * (first_col + block_cols),
                     ]
                     .bitcast(I32)
                     .rearrange("g p b -> p g b"),
                 )
-                for i in range(passes_per_load):
+                if table == 0 and n >= 2:
+                    for first, r in kv_rows[:2]:
+                        load_scale_rows(kv_planes, PLANE_COLS, first, r)
+                    kv_rows = kv_rows[2:]
+                for i in range(load_passes):
                     g = first_pass + i
                     for b in range(banks):
                         byte0 = WORD_BYTES * (i * block_cols + b * BANK_COLS)
-                        col0 = first_col + b * BANK_COLS
+                        col0 = first_col % PLANE_COLS + b * BANK_COLS
                         nc.tensor.matmul_mx(
                             out=accs[b][:],
                             lhsT=x_codes[:, g * TOKENS : (g + 1) * TOKENS].bitcast(FP8X4),
@@ -215,16 +241,21 @@ def tile_gemmaattention_pa_k_kernel(
                             start=(g == 0),
                             stop=(g == PASSES - 1),
                         )
-            for b in range(banks):
-                out_rows = out_block[:, b * HEADS_PER_BANK : (b + 1) * HEADS_PER_BANK, :]
-                if table is not None:
-                    norm_and_rope(nc, work, accs[b], rope_direct[:, table, :, :], rope_crossed[:, table, :, :], out_rows)
-                else:
-                    values = work.tile([P, HEADS_PER_BANK, HEAD], F32)
+                first_pass += load_passes
+            rows = [out_block[:, b * HEADS_PER_BANK : (b + 1) * HEADS_PER_BANK, :] for b in range(banks)]
+            if table is not None:
+                pending = square_and_rotate(accs[0], table)
+                for b in range(banks):
+                    after = square_and_rotate(accs[b + 1], table) if b + 1 < banks else None
+                    scale_and_store(*pending, rows[b])
+                    pending = after
+            else:
+                for b in range(banks):
+                    values = work.tile([P, HEADS_PER_BANK, HEAD], F32, name="values")
                     flat = values[:].rearrange("p h d -> p (h d)")
                     if b % 2 == 0:
                         nc.scalar.copy(out=flat, in_=accs[b][:])
-                        nc.scalar.dma_start(out=out_rows, in_=values[:])
+                        nc.scalar.dma_start(out=rows[b], in_=values[:])
                     else:
                         nc.vector.tensor_copy(out=flat, in_=accs[b][:])
-                        nc.sync.dma_start(out=out_rows, in_=values[:])
+                        nc.sync.dma_start(out=rows[b], in_=values[:])

@@ -31,9 +31,7 @@ EPS = 1e-6
 X_LOADS = 4
 PASSES_PER_BANK = 2
 PASSES_PER_QUANTISE = 4
-PLANE_COLS = 2048
-PLANE_PASSES = 8
-ZERO_PASSES = 4
+PLANE_PASSES = 4
 LOAD_BYTES = 8192
 WORD_BUFS = 8
 WORK_BUFS = 3
@@ -56,41 +54,30 @@ def tile_gemmaattention_pa_k_kernel(
         x_cols = HIDDEN // X_LOADS
         for c in range(X_LOADS):
             cols = slice(c * x_cols, (c + 1) * x_cols)
-            nc.scalar.dma_start(out=x_sb[:, cols], in_=hidden_states[:, cols])
-
+            nc.sync.dma_start(out=x_sb[:, cols], in_=hidden_states[:, cols])
         ident = keep.tile([P, P], F32)
         make_identity(nc, ident[:])
         ones = keep.tile([P, P], BF16)
         nc.gpsimd.memset(ones[:], 1.0)
         gain_rows = keep.tile([P, 2, HEAD], BF16)
         nc.gpsimd.memset(gain_rows[:], 0.0)
-        nc.gpsimd.dma_start(out=gain_rows[0:1, 0, :], in_=q_norm_w.rearrange("(o d) -> o d", o=1))
-        nc.gpsimd.dma_start(out=gain_rows[0:1, 1, :], in_=k_norm_w.rearrange("(o d) -> o d", o=1))
+        nc.scalar.dma_start(out=gain_rows[0:1, 0, :], in_=q_norm_w.rearrange("(o d) -> o d", o=1))
+        nc.scalar.dma_start(out=gain_rows[0:1, 1, :], in_=k_norm_w.rearrange("(o d) -> o d", o=1))
         cos_sb = keep.tile([P, 2, HALF], BF16)
-        nc.gpsimd.dma_start(out=cos_sb[:], in_=cos.rearrange("r (s d) -> r s d", s=2))
+        nc.scalar.dma_start(out=cos_sb[:], in_=cos.rearrange("r (s d) -> r s d", s=2))
         sin_sb = keep.tile([P, 2, HALF], BF16)
-        nc.gpsimd.dma_start(out=sin_sb[:], in_=sin.rearrange("r (s d) -> r s d", s=2))
+        nc.scalar.dma_start(out=sin_sb[:], in_=sin.rearrange("r (s d) -> r s d", s=2))
 
-        q_planes = keep.tile([P, PASSES, PLANE_COLS], U8, align_bytes=64)
-        kv_planes = keep.tile([P, PASSES, PLANE_COLS], U8, align_bytes=64)
+        planes = [
+            keep.tile([P, PLANE_PASSES, COLS], U8, align_bytes=64, name="planes_%d" % s)
+            for s in range(PASSES // PLANE_PASSES)
+        ]
 
-        def zero_planes(planes):
-            for first in range(0, PASSES, ZERO_PASSES):
-                nc.vector.memset(planes[:, first : first + ZERO_PASSES, :].bitcast(I32), 0)
+        def zero_planes(s):
+            nc.vector.memset(planes[s][:].bitcast(I32), 0)
 
-        def load_scale_rows(planes, first_col, first, r):
-            step = slice(first, first + PLANE_PASSES)
-            nc.sync.dma_start(
-                out=planes[r:P:32, step, :].bitcast(I32),
-                in_=w_qkv_scales[step, r:16:4, first_col : first_col + PLANE_COLS]
-                .bitcast(I32)
-                .rearrange("g q n -> q g n"),
-            )
-
-        zero_planes(q_planes)
-        for first in range(0, PASSES, PLANE_PASSES):
-            for r in range(4):
-                load_scale_rows(q_planes, 0, first, r)
+        zero_planes(0)
+        zero_planes(1)
 
         x_words = x_sb[:].bitcast(F32)
         grouped = keep.tile([P, PASSES * TOKENS * 4], BF16, align_bytes=64)
@@ -124,7 +111,15 @@ def tile_gemmaattention_pa_k_kernel(
             if c > 0:
                 quantise(c - 1)
         quantise(PASSES // PASSES_PER_QUANTISE - 1)
-        zero_planes(kv_planes)
+        zero_planes(2)
+        zero_planes(3)
+        for s in range(PASSES // PLANE_PASSES):
+            step = slice(s * PLANE_PASSES, (s + 1) * PLANE_PASSES)
+            for r in range(4):
+                nc.sync.dma_start(
+                    out=planes[s][r:P:32, :, :].bitcast(I32),
+                    in_=w_qkv_scales[step, r:16:4, :].bitcast(I32).rearrange("g q n -> q g n"),
+                )
 
         gain_ps = psum.tile([P, BANK_COLS], F32, tag="bank", name="gain_ps")
         nc.tensor.matmul(
@@ -201,16 +196,14 @@ def tile_gemmaattention_pa_k_kernel(
             (out_1, Q_HEADS * HEAD, K_HEADS, 1, (4,) * 4),
             (out_2, (Q_HEADS + K_HEADS) * HEAD, V_HEADS, None, (4, 4, 4, 2, 1, 1)),
         )
-        kv_rows = [(first, r) for first in range(0, PASSES, PLANE_PASSES) for r in range(4)]
         for out_block, first_col, heads, table, loads in blocks:
             block_cols = heads * HEAD
             banks = block_cols // BANK_COLS
-            planes = q_planes if first_col < PLANE_COLS else kv_planes
             accs = [
                 psum.tile([P, BANK_COLS], F32, tag="bank", name="acc_%d_%d" % (first_col, b)) for b in range(banks)
             ]
             first_pass = 0
-            for n, load_passes in enumerate(loads):
+            for load_passes in loads:
                 load_bytes = load_passes * WORD_BYTES * block_cols
                 words = stream.tile([P, LOAD_BYTES], U8, align_bytes=64, name="words")
                 nc.sync.dma_start(
@@ -223,21 +216,17 @@ def tile_gemmaattention_pa_k_kernel(
                     .bitcast(I32)
                     .rearrange("g p b -> p g b"),
                 )
-                if table == 0 and n >= 2:
-                    for first, r in kv_rows[:2]:
-                        load_scale_rows(kv_planes, PLANE_COLS, first, r)
-                    kv_rows = kv_rows[2:]
                 for i in range(load_passes):
                     g = first_pass + i
                     for b in range(banks):
                         byte0 = WORD_BYTES * (i * block_cols + b * BANK_COLS)
-                        col0 = first_col % PLANE_COLS + b * BANK_COLS
+                        col0 = first_col + b * BANK_COLS
                         nc.tensor.matmul_mx(
                             out=accs[b][:],
                             lhsT=x_codes[:, g * TOKENS : (g + 1) * TOKENS].bitcast(FP8X4),
                             lhsT_scale=x_scales[:, g * TOKENS : (g + 1) * TOKENS],
                             rhs=words[:, byte0 : byte0 + WORD_BYTES * BANK_COLS].bitcast(FP4X4),
-                            rhs_scale=planes[:, g, col0 : col0 + BANK_COLS],
+                            rhs_scale=planes[g // PLANE_PASSES][:, g % PLANE_PASSES, col0 : col0 + BANK_COLS],
                             start=(g == 0),
                             stop=(g == PASSES - 1),
                         )

@@ -28,10 +28,11 @@ HEADS_PER_BANK = BANK_COLS // HEAD
 WORD_BYTES = 2
 EPS = 1e-6
 
-X_LOADS = 4
+X_LOADS = 2
 PASSES_PER_BANK = 2
 PASSES_PER_QUANTISE = 4
-PLANE_PASSES = 4
+PLANE_GROUPS = (4, 8, 4)
+FRONT_LOADS = 3
 LOAD_BYTES = 8192
 WORD_BUFS = 8
 WORK_BUFS = 3
@@ -68,13 +69,23 @@ def tile_gemmaattention_pa_k_kernel(
         sin_sb = keep.tile([P, 2, HALF], BF16)
         nc.scalar.dma_start(out=sin_sb[:], in_=sin.rearrange("r (s d) -> r s d", s=2))
 
+        group_of = [(s, i) for s, size in enumerate(PLANE_GROUPS) for i in range(size)]
         planes = [
-            keep.tile([P, PLANE_PASSES, COLS], U8, align_bytes=64, name="planes_%d" % s)
-            for s in range(PASSES // PLANE_PASSES)
+            keep.tile([P, size, COLS], U8, align_bytes=64, name="planes_%d" % s) for s, size in enumerate(PLANE_GROUPS)
         ]
 
         def zero_planes(s):
             nc.vector.memset(planes[s][:].bitcast(I32), 0)
+
+        def load_scale_rows(s):
+            first = sum(PLANE_GROUPS[:s])
+            step = slice(first, first + PLANE_GROUPS[s])
+            for q in range(8):
+                part = 32 * (q // 4) + q % 4
+                nc.sync.dma_start(
+                    out=planes[s][part:P:64, :, :].bitcast(I32),
+                    in_=w_qkv_scales[step, q:16:8, :].bitcast(I32).rearrange("g q n -> q g n"),
+                )
 
         zero_planes(0)
         zero_planes(1)
@@ -112,14 +123,6 @@ def tile_gemmaattention_pa_k_kernel(
                 quantise(c - 1)
         quantise(PASSES // PASSES_PER_QUANTISE - 1)
         zero_planes(2)
-        zero_planes(3)
-        for s in range(PASSES // PLANE_PASSES):
-            step = slice(s * PLANE_PASSES, (s + 1) * PLANE_PASSES)
-            for r in range(4):
-                nc.sync.dma_start(
-                    out=planes[s][r:P:32, :, :].bitcast(I32),
-                    in_=w_qkv_scales[step, r:16:4, :].bitcast(I32).rearrange("g q n -> q g n"),
-                )
 
         gain_ps = psum.tile([P, BANK_COLS], F32, tag="bank", name="gain_ps")
         nc.tensor.matmul(
@@ -191,6 +194,22 @@ def tile_gemmaattention_pa_k_kernel(
                 )
             nc.scalar.dma_start(out=out_rows, in_=rotated[:])
 
+        def load_words(first_pass, load_passes, first_col, block_cols):
+            words = stream.tile([P, LOAD_BYTES], U8, align_bytes=64, name="words")
+            nc.sync.dma_start(
+                out=words[:, : load_passes * WORD_BYTES * block_cols]
+                .bitcast(I32)
+                .rearrange("p (g b) -> p g b", g=load_passes),
+                in_=w_qkv_words[
+                    first_pass : first_pass + load_passes,
+                    :,
+                    WORD_BYTES * first_col : WORD_BYTES * (first_col + block_cols),
+                ]
+                .bitcast(I32)
+                .rearrange("g p b -> p g b"),
+            )
+            return words
+
         blocks = (
             (out_0, 0, Q_HEADS, 0, (2,) * 8),
             (out_1, Q_HEADS * HEAD, K_HEADS, 1, (4,) * 4),
@@ -202,22 +221,18 @@ def tile_gemmaattention_pa_k_kernel(
             accs = [
                 psum.tile([P, BANK_COLS], F32, tag="bank", name="acc_%d_%d" % (first_col, b)) for b in range(banks)
             ]
-            first_pass = 0
-            for load_passes in loads:
-                load_bytes = load_passes * WORD_BYTES * block_cols
-                words = stream.tile([P, LOAD_BYTES], U8, align_bytes=64, name="words")
-                nc.sync.dma_start(
-                    out=words[:, :load_bytes].bitcast(I32).rearrange("p (g b) -> p g b", g=load_passes),
-                    in_=w_qkv_words[
-                        first_pass : first_pass + load_passes,
-                        :,
-                        WORD_BYTES * first_col : WORD_BYTES * (first_col + block_cols),
-                    ]
-                    .bitcast(I32)
-                    .rearrange("g p b -> p g b"),
-                )
+            first_passes = [sum(loads[:n]) for n in range(len(loads))]
+            pieces = []
+            for n, load_passes in enumerate(loads):
+                while len(pieces) < max(n + 1, FRONT_LOADS if table == 0 else 0):
+                    pieces.append(load_words(first_passes[len(pieces)], loads[len(pieces)], first_col, block_cols))
+                    if table == 0 and len(pieces) == FRONT_LOADS:
+                        for s in range(len(PLANE_GROUPS)):
+                            load_scale_rows(s)
+                words = pieces[n]
                 for i in range(load_passes):
-                    g = first_pass + i
+                    g = first_passes[n] + i
+                    s, place = group_of[g]
                     for b in range(banks):
                         byte0 = WORD_BYTES * (i * block_cols + b * BANK_COLS)
                         col0 = first_col + b * BANK_COLS
@@ -226,11 +241,10 @@ def tile_gemmaattention_pa_k_kernel(
                             lhsT=x_codes[:, g * TOKENS : (g + 1) * TOKENS].bitcast(FP8X4),
                             lhsT_scale=x_scales[:, g * TOKENS : (g + 1) * TOKENS],
                             rhs=words[:, byte0 : byte0 + WORD_BYTES * BANK_COLS].bitcast(FP4X4),
-                            rhs_scale=planes[g // PLANE_PASSES][:, g % PLANE_PASSES, col0 : col0 + BANK_COLS],
+                            rhs_scale=planes[s][:, place, col0 : col0 + BANK_COLS],
                             start=(g == 0),
                             stop=(g == PASSES - 1),
                         )
-                first_pass += load_passes
             rows = [out_block[:, b * HEADS_PER_BANK : (b + 1) * HEADS_PER_BANK, :] for b in range(banks)]
             if table is not None:
                 pending = square_and_rotate(accs[0], table)

@@ -31,8 +31,8 @@ EPS = 1e-6
 X_LOADS = 2
 PASSES_PER_BANK = 2
 PASSES_PER_QUANTISE = 4
-PLANE_GROUPS = (4, 8, 4)
-FRONT_LOADS = 3
+PLANE_GROUPS = (4, 4, 4, 2, 2)
+FRONT_LOADS = 6
 LOAD_BYTES = 8192
 WORD_BUFS = 8
 WORK_BUFS = 3
@@ -56,6 +56,11 @@ def tile_gemmaattention_pa_k_kernel(
         for c in range(X_LOADS):
             cols = slice(c * x_cols, (c + 1) * x_cols)
             nc.sync.dma_start(out=x_sb[:, cols], in_=hidden_states[:, cols])
+        eps_col = keep.tile([P, 1], F32)
+        nc.gpsimd.memset(eps_col[:], 0.0)
+        nc.gpsimd.tensor_scalar(out=eps_col[:], in0=eps_col[:], scalar1=1.0, scalar2=EPS, op0=ALU.mult, op1=ALU.add)
+        table_load = keep.tile([P, 1], F32)
+        nc.scalar.activation(out=table_load[:], in_=eps_col[:], func=ACT.Abs_reciprocal_sqrt)
         ident = keep.tile([P, P], F32)
         make_identity(nc, ident[:])
         ones = keep.tile([P, P], BF16)
@@ -88,7 +93,6 @@ def tile_gemmaattention_pa_k_kernel(
                 )
 
         zero_planes(0)
-        zero_planes(1)
 
         x_words = x_sb[:].bitcast(F32)
         grouped = keep.tile([P, PASSES * TOKENS * 4], BF16, align_bytes=64)
@@ -122,7 +126,8 @@ def tile_gemmaattention_pa_k_kernel(
             if c > 0:
                 quantise(c - 1)
         quantise(PASSES // PASSES_PER_QUANTISE - 1)
-        zero_planes(2)
+        for s in range(1, len(PLANE_GROUPS)):
+            zero_planes(s)
 
         gain_ps = psum.tile([P, BANK_COLS], F32, tag="bank", name="gain_ps")
         nc.tensor.matmul(
@@ -146,8 +151,7 @@ def tile_gemmaattention_pa_k_kernel(
                 op=ALU.mult,
             )
 
-        def square_and_rotate(acc, table):
-            by_half = acc[:].rearrange("p (h s d) -> p h s d", h=HEADS_PER_BANK, s=2)
+        def norm_and_rope(acc, table, name):
             squares = work.tile([P, HEAD], F32, name="squares")
             sumsq = work.tile([P, HEADS_PER_BANK], F32, name="sumsq")
             for h in range(HEADS_PER_BANK):
@@ -157,10 +161,22 @@ def tile_gemmaattention_pa_k_kernel(
                     func=ACT.Square,
                     accum_out=sumsq[:, h : h + 1],
                 )
+            rstd = work.tile([P, HEADS_PER_BANK], F32, name="rstd")
+            nc.scalar.activation(
+                out=rstd[:], in_=sumsq[:], func=ACT.Abs_reciprocal_sqrt, scale=1.0 / HEAD, bias=eps_col[:]
+            )
+            normed = work.tile([P, HEADS_PER_BANK, 2, HALF], F32, name="normed")
+            for h in range(HEADS_PER_BANK):
+                nc.scalar.activation(
+                    out=normed[:, h, :, :].rearrange("p s d -> p (s d)"),
+                    in_=acc[:, h * HEAD : (h + 1) * HEAD],
+                    func=ACT.Copy,
+                    scale=rstd[:, h : h + 1],
+                )
             direct = work.tile([P, HEADS_PER_BANK, 2, HALF], F32, name="direct")
             nc.vector.tensor_tensor(
                 out=direct[:],
-                in0=by_half,
+                in0=normed[:],
                 in1=rope_direct[:, table, :, :].unsqueeze(1).to_broadcast([P, HEADS_PER_BANK, 2, HALF]),
                 op=ALU.mult,
             )
@@ -168,97 +184,79 @@ def tile_gemmaattention_pa_k_kernel(
             for s in range(2):
                 nc.vector.tensor_tensor(
                     out=crossed[:, :, s, :],
-                    in0=by_half[:, :, 1 - s, :],
+                    in0=normed[:, :, 1 - s, :],
                     in1=rope_crossed[:, table, s, :].unsqueeze(1).to_broadcast([P, HEADS_PER_BANK, HALF]),
                     op=ALU.mult,
                 )
-            mean_sq = work.tile([P, HEADS_PER_BANK], F32, name="mean_sq")
-            nc.vector.tensor_scalar(
-                out=mean_sq[:], in0=sumsq[:], scalar1=1.0 / HEAD, scalar2=EPS, op0=ALU.mult, op1=ALU.add
-            )
-            return direct, crossed, mean_sq
+            result = keep.tile([P, HEADS_PER_BANK, 2, HALF], F32, name=name)
+            nc.vector.tensor_tensor(out=result[:], in0=direct[:], in1=crossed[:], op=ALU.add)
+            return result
 
-        def scale_and_store(direct, crossed, mean_sq, out_rows):
-            root = work.tile([P, HEADS_PER_BANK], F32, name="root")
-            nc.scalar.activation(out=root[:], in_=mean_sq[:], func=ACT.Sqrt)
-            nc.vector.tensor_tensor(out=direct[:], in0=direct[:], in1=crossed[:], op=ALU.add)
-            rstd = work.tile([P, HEADS_PER_BANK], F32, name="rstd")
-            nc.vector.reciprocal(out=rstd[:], in_=root[:])
-            rotated = work.tile([P, HEADS_PER_BANK, HEAD], F32, name="rotated")
-            for h in range(HEADS_PER_BANK):
-                nc.scalar.activation(
-                    out=rotated[:, h, :],
-                    in_=direct[:, h, :, :].rearrange("p s d -> p (s d)"),
-                    func=ACT.Copy,
-                    scale=rstd[:, h : h + 1],
-                )
-            nc.scalar.dma_start(out=out_rows, in_=rotated[:])
-
-        def load_words(first_pass, load_passes, first_col, block_cols):
+        def load_words(first_pass, load_passes, first_col, cols):
             words = stream.tile([P, LOAD_BYTES], U8, align_bytes=64, name="words")
             nc.sync.dma_start(
-                out=words[:, : load_passes * WORD_BYTES * block_cols]
-                .bitcast(I32)
-                .rearrange("p (g b) -> p g b", g=load_passes),
+                out=words[:, : load_passes * WORD_BYTES * cols].bitcast(I32).rearrange("p (g b) -> p g b", g=load_passes),
                 in_=w_qkv_words[
-                    first_pass : first_pass + load_passes,
-                    :,
-                    WORD_BYTES * first_col : WORD_BYTES * (first_col + block_cols),
+                    first_pass : first_pass + load_passes, :, WORD_BYTES * first_col : WORD_BYTES * (first_col + cols)
                 ]
                 .bitcast(I32)
                 .rearrange("g p b -> p g b"),
             )
             return words
 
-        blocks = (
-            (out_0, 0, Q_HEADS, 0, (2,) * 8),
-            (out_1, Q_HEADS * HEAD, K_HEADS, 1, (4,) * 4),
-            (out_2, (Q_HEADS + K_HEADS) * HEAD, V_HEADS, None, (4, 4, 4, 2, 1, 1)),
-        )
-        for out_block, first_col, heads, table, loads in blocks:
-            block_cols = heads * HEAD
-            banks = block_cols // BANK_COLS
-            accs = [
-                psum.tile([P, BANK_COLS], F32, tag="bank", name="acc_%d_%d" % (first_col, b)) for b in range(banks)
-            ]
-            first_passes = [sum(loads[:n]) for n in range(len(loads))]
-            pieces = []
-            for n, load_passes in enumerate(loads):
-                while len(pieces) < max(n + 1, FRONT_LOADS if table == 0 else 0):
-                    pieces.append(load_words(first_passes[len(pieces)], loads[len(pieces)], first_col, block_cols))
-                    if table == 0 and len(pieces) == FRONT_LOADS:
-                        for s in range(len(PLANE_GROUPS)):
-                            load_scale_rows(s)
-                words = pieces[n]
-                for i in range(load_passes):
-                    g = first_passes[n] + i
-                    s, place = group_of[g]
-                    for b in range(banks):
-                        byte0 = WORD_BYTES * (i * block_cols + b * BANK_COLS)
-                        col0 = first_col + b * BANK_COLS
-                        nc.tensor.matmul_mx(
-                            out=accs[b][:],
-                            lhsT=x_codes[:, g * TOKENS : (g + 1) * TOKENS].bitcast(FP8X4),
-                            lhsT_scale=x_scales[:, g * TOKENS : (g + 1) * TOKENS],
-                            rhs=words[:, byte0 : byte0 + WORD_BYTES * BANK_COLS].bitcast(FP4X4),
-                            rhs_scale=planes[s][:, place, col0 : col0 + BANK_COLS],
-                            start=(g == 0),
-                            stop=(g == PASSES - 1),
-                        )
-            rows = [out_block[:, b * HEADS_PER_BANK : (b + 1) * HEADS_PER_BANK, :] for b in range(banks)]
-            if table is not None:
-                pending = square_and_rotate(accs[0], table)
-                for b in range(banks):
-                    after = square_and_rotate(accs[b + 1], table) if b + 1 < banks else None
-                    scale_and_store(*pending, rows[b])
-                    pending = after
+        def multiply(words, first_pass, load_passes, first_col, cols):
+            for i in range(load_passes):
+                g = first_pass + i
+                s, place = group_of[g]
+                for c in range(0, cols, BANK_COLS):
+                    byte0 = WORD_BYTES * (i * cols + c)
+                    nc.tensor.matmul_mx(
+                        out=accs[(first_col + c) // BANK_COLS][:],
+                        lhsT=x_codes[:, g * TOKENS : (g + 1) * TOKENS].bitcast(FP8X4),
+                        lhsT_scale=x_scales[:, g * TOKENS : (g + 1) * TOKENS],
+                        rhs=words[:, byte0 : byte0 + WORD_BYTES * BANK_COLS].bitcast(FP4X4),
+                        rhs_scale=planes[s][:, place, first_col + c : first_col + c + BANK_COLS],
+                        start=(g == 0),
+                        stop=(g == PASSES - 1),
+                    )
+
+        q_cols, k_cols, v_cols = Q_HEADS * HEAD, K_HEADS * HEAD, V_HEADS * HEAD
+        accs = [psum.tile([P, BANK_COLS], F32, tag="bank", name="acc_%d" % b) for b in range(COLS // BANK_COLS)]
+        q_banks, k_banks = q_cols // BANK_COLS, k_cols // BANK_COLS
+
+        load_scale_rows(0)
+        q_loads = [(first, 2, 0, q_cols) for first in range(0, PASSES, 2)]
+        q_words = [load_words(*load) for load in q_loads[:FRONT_LOADS]]
+        for s in range(1, len(PLANE_GROUPS)):
+            load_scale_rows(s)
+        q_words += [load_words(*load) for load in q_loads[FRONT_LOADS:]]
+        for words, load in zip(q_words, q_loads):
+            multiply(words, *load)
+        q_results = [norm_and_rope(acc, 0, "q_result_%d" % b) for b, acc in enumerate(accs[:q_banks])]
+
+        for load in [(first, 2, q_cols, k_cols + v_cols) for first in range(0, 4, 2)] + [
+            (first, 4, q_cols, k_cols) for first in range(4, PASSES, 4)
+        ]:
+            multiply(load_words(*load), *load)
+        k_accs = accs[q_banks : q_banks + k_banks]
+        k_results = [norm_and_rope(acc, 1, "k_result_%d" % b) for b, acc in enumerate(k_accs)]
+        for first, load_passes in ((4, 4), (8, 4), (12, 2), (14, 1), (15, 1)):
+            load = (first, load_passes, q_cols + k_cols, v_cols)
+            multiply(load_words(*load), *load)
+
+        for out, results in ((out_0, q_results), (out_1, k_results)):
+            for b, result in enumerate(results):
+                nc.sync.dma_start(
+                    out=out[:, b * HEADS_PER_BANK : (b + 1) * HEADS_PER_BANK, :],
+                    in_=result[:].rearrange("p h s d -> p h (s d)"),
+                )
+        for b, acc in enumerate(accs[q_banks + k_banks :]):
+            values = work.tile([P, HEADS_PER_BANK, HEAD], F32, name="values")
+            flat = values[:].rearrange("p h d -> p (h d)")
+            rows = out_2[:, b * HEADS_PER_BANK : (b + 1) * HEADS_PER_BANK, :]
+            if b % 2 == 0:
+                nc.scalar.copy(out=flat, in_=acc[:])
+                nc.scalar.dma_start(out=rows, in_=values[:])
             else:
-                for b in range(banks):
-                    values = work.tile([P, HEADS_PER_BANK, HEAD], F32, name="values")
-                    flat = values[:].rearrange("p h d -> p (h d)")
-                    if b % 2 == 0:
-                        nc.scalar.copy(out=flat, in_=accs[b][:])
-                        nc.scalar.dma_start(out=rows[b], in_=values[:])
-                    else:
-                        nc.vector.tensor_copy(out=flat, in_=accs[b][:])
-                        nc.sync.dma_start(out=rows[b], in_=values[:])
+                nc.vector.tensor_copy(out=flat, in_=acc[:])
+                nc.sync.dma_start(out=rows, in_=values[:])

@@ -31,8 +31,8 @@ EPS = 1e-6
 X_LOADS = 2
 PASSES_PER_BANK = 2
 PASSES_PER_QUANTISE = 4
-PLANE_GROUPS = (4, 4, 4, 2, 2)
-FRONT_LOADS = 6
+PLANE_GROUPS = (4, 4, 4, 3, 1)
+FRONT_LOADS = 5
 LOAD_BYTES = 8192
 WORD_BUFS = 8
 WORK_BUFS = 3
@@ -224,10 +224,9 @@ def tile_gemmaattention_pa_k_kernel(
         accs = [psum.tile([P, BANK_COLS], F32, tag="bank", name="acc_%d" % b) for b in range(COLS // BANK_COLS)]
         q_banks, k_banks = q_cols // BANK_COLS, k_cols // BANK_COLS
 
-        load_scale_rows(0)
         q_loads = [(first, 2, 0, q_cols) for first in range(0, PASSES, 2)]
         q_words = [load_words(*load) for load in q_loads[:FRONT_LOADS]]
-        for s in range(1, len(PLANE_GROUPS)):
+        for s in range(len(PLANE_GROUPS)):
             load_scale_rows(s)
         q_words += [load_words(*load) for load in q_loads[FRONT_LOADS:]]
         for words, load in zip(q_words, q_loads):

@@ -32,9 +32,9 @@ X_LOADS = 2
 PASSES_PER_BANK = 2
 PASSES_PER_QUANTISE = 4
 PLANE_GROUPS = (4, 4, 4, 3, 1)
-FRONT_LOADS = 5
-LOAD_BYTES = 8192
-WORD_BUFS = 8
+FRONT_LOADS = 10
+LOAD_BYTES = 4096
+WORD_BUFS = 16
 WORK_BUFS = 3
 
 FLOPS = 2 * TOKENS * HIDDEN * COLS
@@ -224,7 +224,7 @@ def tile_gemmaattention_pa_k_kernel(
         accs = [psum.tile([P, BANK_COLS], F32, tag="bank", name="acc_%d" % b) for b in range(COLS // BANK_COLS)]
         q_banks, k_banks = q_cols // BANK_COLS, k_cols // BANK_COLS
 
-        q_loads = [(first, 2, 0, q_cols) for first in range(0, PASSES, 2)]
+        q_loads = [(g, 1, 0, q_cols) for g in range(PASSES)]
         q_words = [load_words(*load) for load in q_loads[:FRONT_LOADS]]
         for s in range(len(PLANE_GROUPS)):
             load_scale_rows(s)
@@ -233,14 +233,18 @@ def tile_gemmaattention_pa_k_kernel(
             multiply(words, *load)
         q_results = [norm_and_rope(acc, 0, "q_result_%d" % b) for b, acc in enumerate(accs[:q_banks])]
 
-        for load in [(first, 2, q_cols, k_cols + v_cols) for first in range(0, 4, 2)] + [
-            (first, 4, q_cols, k_cols) for first in range(4, PASSES, 4)
+        for load in [(g, 1, q_cols, k_cols + v_cols) for g in range(4)] + [
+            (first, 2, q_cols, k_cols) for first in range(4, PASSES, 2)
         ]:
             multiply(load_words(*load), *load)
         k_accs = accs[q_banks : q_banks + k_banks]
         k_results = [norm_and_rope(acc, 1, "k_result_%d" % b) for b, acc in enumerate(k_accs)]
-        for first, load_passes in ((4, 4), (8, 4), (12, 2), (14, 1), (15, 1)):
-            load = (first, load_passes, q_cols + k_cols, v_cols)
+        v_col = q_cols + k_cols
+        for load in (
+            [(first, 2, v_col, v_cols) for first in range(4, PASSES - 2, 2)]
+            + [(PASSES - 2, 1, v_col, v_cols)]
+            + [(PASSES - 1, 1, col, BANK_COLS) for col in range(v_col, COLS, BANK_COLS)]
+        ):
             multiply(load_words(*load), *load)
 
         for out, results in ((out_0, q_results), (out_1, k_results)):

from contextlib import ExitStack

import concourse.mybir as mybir
from concourse.masks import make_identity

F32 = mybir.dt.float32
BF16 = mybir.dt.bfloat16
I32 = mybir.dt.int32
U8 = mybir.dt.uint8
U32 = mybir.dt.uint32
FP8X4 = mybir.dt.float8_e4m3fn_x4
FP4X4 = mybir.dt.float4_e2m1fn_x4
ACT = mybir.ActivationFunctionType
ALU = mybir.AluOpType

P = 128
TOKENS = 128
HIDDEN = 8192
K_PASS = 512
PASSES = HIDDEN // K_PASS
HEAD = 256
HALF = HEAD // 2
Q_HEADS, K_HEADS, V_HEADS = 8, 4, 4
COLS = (Q_HEADS + K_HEADS + V_HEADS) * HEAD
BANK_COLS = 512
PSUM_BANKS = 8
HEADS_PER_BANK = BANK_COLS // HEAD
WORD_BYTES = 2
EPS = 1e-6

X_LOADS = 2
PASSES_PER_BANK = 2
PASSES_PER_QUANTISE = 4
PLANE_GROUPS = (4, 4, 4, 3, 1)
FRONT_LOADS = 10
LOAD_BYTES = 4096
WORD_BUFS = 16
WORK_BUFS = 3

FLOPS = 2 * TOKENS * HIDDEN * COLS


def tile_gemmaattention_pa_k_kernel(
    tc, hidden_states, w_qkv_words, w_qkv_scales, q_norm_w, k_norm_w, cos, sin, out_0, out_1, out_2
):
    nc = tc.nc
    with ExitStack() as ctx:
        keep = ctx.enter_context(tc.tile_pool(name="keep", bufs=1))
        stream = ctx.enter_context(tc.tile_pool(name="stream", bufs=WORD_BUFS))
        work = ctx.enter_context(tc.tile_pool(name="work", bufs=WORK_BUFS))
        psum = ctx.enter_context(tc.psum_pool(name="psum", bufs=PSUM_BANKS))
        ctx.enter_context(tc.manual_schedule())

        x_sb = keep.tile([P, HIDDEN], BF16)
        x_cols = HIDDEN // X_LOADS
        for c in range(X_LOADS):
            cols = slice(c * x_cols, (c + 1) * x_cols)
            nc.sync.dma_start(out=x_sb[:, cols], in_=hidden_states[:, cols])
        eps_col = keep.tile([P, 1], F32)
        nc.gpsimd.memset(eps_col[:], 0.0)
        nc.gpsimd.tensor_scalar(out=eps_col[:], in0=eps_col[:], scalar1=1.0, scalar2=EPS, op0=ALU.mult, op1=ALU.add)
        table_load = keep.tile([P, 1], F32)
        nc.scalar.activation(out=table_load[:], in_=eps_col[:], func=ACT.Abs_reciprocal_sqrt)
        ident = keep.tile([P, P], F32)
        make_identity(nc, ident[:])
        ones = keep.tile([P, P], BF16)
        nc.gpsimd.memset(ones[:], 1.0)
        gain_rows = keep.tile([P, 2, HEAD], BF16)
        nc.gpsimd.memset(gain_rows[:], 0.0)
        nc.scalar.dma_start(out=gain_rows[0:1, 0, :], in_=q_norm_w.rearrange("(o d) -> o d", o=1))
        nc.scalar.dma_start(out=gain_rows[0:1, 1, :], in_=k_norm_w.rearrange("(o d) -> o d", o=1))
        cos_sb = keep.tile([P, 2, HALF], BF16)
        nc.scalar.dma_start(out=cos_sb[:], in_=cos.rearrange("r (s d) -> r s d", s=2))
        sin_sb = keep.tile([P, 2, HALF], BF16)
        nc.scalar.dma_start(out=sin_sb[:], in_=sin.rearrange("r (s d) -> r s d", s=2))

        group_of = [(s, i) for s, size in enumerate(PLANE_GROUPS) for i in range(size)]
        planes = [
            keep.tile([P, size, COLS], U8, align_bytes=64, name="planes_%d" % s) for s, size in enumerate(PLANE_GROUPS)
        ]

        def zero_planes(s):
            nc.vector.memset(planes[s][:].bitcast(I32), 0)

        def load_scale_rows(s):
            first = sum(PLANE_GROUPS[:s])
            step = slice(first, first + PLANE_GROUPS[s])
            for q in range(8):
                part = 32 * (q // 4) + q % 4
                nc.sync.dma_start(
                    out=planes[s][part:P:64, :, :].bitcast(I32),
                    in_=w_qkv_scales[step, q:16:8, :].bitcast(I32).rearrange("g q n -> q g n"),
                )

        zero_planes(0)

        x_words = x_sb[:].bitcast(F32)
        grouped = keep.tile([P, PASSES * TOKENS * 4], BF16, align_bytes=64)
        grouped_words = grouped[:].bitcast(F32).rearrange("p (g r u) -> p g r u", g=PASSES, u=2)
        x_codes = keep.tile([P, PASSES * TOKENS], U32, align_bytes=64)
        x_scales = keep.tile([P, PASSES * TOKENS], U8, align_bytes=64)

        def transpose_bank(j):
            xt = psum.tile([P, PASSES_PER_BANK, 2, TOKENS], F32, tag="bank", name="xt_%d" % j)
            for i in range(PASSES_PER_BANK):
                g = j * PASSES_PER_BANK + i
                for u in range(2):
                    nc.tensor.transpose(xt[:, i, u, :], x_words[:, 256 * g + u : 256 * (g + 1) : 2], ident[:])
            pair = slice(j * PASSES_PER_BANK, (j + 1) * PASSES_PER_BANK)
            if j % 2 == 0:
                nc.vector.tensor_copy(out=grouped_words[:, pair, :, :], in_=xt[:].rearrange("p g u r -> p g r u"))
            else:
                nc.scalar.copy(out=grouped_words[:, pair, :, :], in_=xt[:].rearrange("p g u r -> p g r u"))

        def quantise(c):
            width = PASSES_PER_QUANTISE * TOKENS
            nc.vector.quantize_mx(
                out=x_codes[:, c * width : (c + 1) * width].bitcast(FP8X4),
                scales=x_scales[:, c * width : (c + 1) * width],
                in_=grouped[:, 4 * c * width : 4 * (c + 1) * width],
            )

        for c in range(PASSES // PASSES_PER_QUANTISE):
            transpose_bank(2 * c)
            transpose_bank(2 * c + 1)
            if c > 0:
                quantise(c - 1)
        quantise(PASSES // PASSES_PER_QUANTISE - 1)
        for s in range(1, len(PLANE_GROUPS)):
            zero_planes(s)

        gain_ps = psum.tile([P, BANK_COLS], F32, tag="bank", name="gain_ps")
        nc.tensor.matmul(
            out=gain_ps[:], lhsT=ones[:], rhs=gain_rows[:].rearrange("p w d -> p (w d)"), start=True, stop=True
        )
        gain = keep.tile([P, 2, 2, HALF], F32)
        nc.vector.tensor_scalar_add(out=gain[:].rearrange("p w s d -> p (w s d)"), in0=gain_ps[:], scalar1=1.0)
        sin_signed = keep.tile([P, 2, HALF], F32)
        nc.vector.tensor_scalar_mul(out=sin_signed[:, 0, :], in0=sin_sb[:, 0, :], scalar1=-1.0)
        nc.vector.tensor_copy(out=sin_signed[:, 1, :], in_=sin_sb[:, 1, :])
        rope_direct = keep.tile([P, 2, 2, HALF], F32)
        nc.vector.tensor_tensor(
            out=rope_direct[:], in0=gain[:], in1=cos_sb[:].unsqueeze(1).to_broadcast([P, 2, 2, HALF]), op=ALU.mult
        )
        rope_crossed = keep.tile([P, 2, 2, HALF], F32)
        for s in range(2):
            nc.vector.tensor_tensor(
                out=rope_crossed[:, :, s, :],
                in0=gain[:, :, 1 - s, :],
                in1=sin_signed[:, s, :].unsqueeze(1).to_broadcast([P, 2, HALF]),
                op=ALU.mult,
            )

        def norm_and_rope(acc, table, name):
            squares = work.tile([P, HEAD], F32, name="squares")
            sumsq = work.tile([P, HEADS_PER_BANK], F32, name="sumsq")
            for h in range(HEADS_PER_BANK):
                nc.scalar.activation(
                    out=squares[:],
                    in_=acc[:, h * HEAD : (h + 1) * HEAD],
                    func=ACT.Square,
                    accum_out=sumsq[:, h : h + 1],
                )
            rstd = work.tile([P, HEADS_PER_BANK], F32, name="rstd")
            nc.scalar.activation(
                out=rstd[:], in_=sumsq[:], func=ACT.Abs_reciprocal_sqrt, scale=1.0 / HEAD, bias=eps_col[:]
            )
            normed = work.tile([P, HEADS_PER_BANK, 2, HALF], F32, name="normed")
            for h in range(HEADS_PER_BANK):
                nc.scalar.activation(
                    out=normed[:, h, :, :].rearrange("p s d -> p (s d)"),
                    in_=acc[:, h * HEAD : (h + 1) * HEAD],
                    func=ACT.Copy,
                    scale=rstd[:, h : h + 1],
                )
            direct = work.tile([P, HEADS_PER_BANK, 2, HALF], F32, name="direct")
            nc.vector.tensor_tensor(
                out=direct[:],
                in0=normed[:],
                in1=rope_direct[:, table, :, :].unsqueeze(1).to_broadcast([P, HEADS_PER_BANK, 2, HALF]),
                op=ALU.mult,
            )
            crossed = work.tile([P, HEADS_PER_BANK, 2, HALF], F32, name="crossed")
            for s in range(2):
                nc.vector.tensor_tensor(
                    out=crossed[:, :, s, :],
                    in0=normed[:, :, 1 - s, :],
                    in1=rope_crossed[:, table, s, :].unsqueeze(1).to_broadcast([P, HEADS_PER_BANK, HALF]),
                    op=ALU.mult,
                )
            result = keep.tile([P, HEADS_PER_BANK, 2, HALF], F32, name=name)
            nc.vector.tensor_tensor(out=result[:], in0=direct[:], in1=crossed[:], op=ALU.add)
            return result

        def load_words(first_pass, load_passes, first_col, cols):
            words = stream.tile([P, LOAD_BYTES], U8, align_bytes=64, name="words")
            nc.sync.dma_start(
                out=words[:, : load_passes * WORD_BYTES * cols].bitcast(I32).rearrange("p (g b) -> p g b", g=load_passes),
                in_=w_qkv_words[
                    first_pass : first_pass + load_passes, :, WORD_BYTES * first_col : WORD_BYTES * (first_col + cols)
                ]
                .bitcast(I32)
                .rearrange("g p b -> p g b"),
            )
            return words

        def multiply(words, first_pass, load_passes, first_col, cols):
            for i in range(load_passes):
                g = first_pass + i
                s, place = group_of[g]
                for c in range(0, cols, BANK_COLS):
                    byte0 = WORD_BYTES * (i * cols + c)
                    nc.tensor.matmul_mx(
                        out=accs[(first_col + c) // BANK_COLS][:],
                        lhsT=x_codes[:, g * TOKENS : (g + 1) * TOKENS].bitcast(FP8X4),
                        lhsT_scale=x_scales[:, g * TOKENS : (g + 1) * TOKENS],
                        rhs=words[:, byte0 : byte0 + WORD_BYTES * BANK_COLS].bitcast(FP4X4),
                        rhs_scale=planes[s][:, place, first_col + c : first_col + c + BANK_COLS],
                        start=(g == 0),
                        stop=(g == PASSES - 1),
                    )

        q_cols, k_cols, v_cols = Q_HEADS * HEAD, K_HEADS * HEAD, V_HEADS * HEAD
        accs = [psum.tile([P, BANK_COLS], F32, tag="bank", name="acc_%d" % b) for b in range(COLS // BANK_COLS)]
        q_banks, k_banks = q_cols // BANK_COLS, k_cols // BANK_COLS

        q_loads = [(g, 1, 0, q_cols) for g in range(PASSES)]
        q_words = [load_words(*load) for load in q_loads[:FRONT_LOADS]]
        for s in range(len(PLANE_GROUPS)):
            load_scale_rows(s)
        q_words += [load_words(*load) for load in q_loads[FRONT_LOADS:]]
        for words, load in zip(q_words, q_loads):
            multiply(words, *load)
        q_results = [norm_and_rope(acc, 0, "q_result_%d" % b) for b, acc in enumerate(accs[:q_banks])]

        for load in [(g, 1, q_cols, k_cols + v_cols) for g in range(4)] + [
            (first, 2, q_cols, k_cols) for first in range(4, PASSES, 2)
        ]:
            multiply(load_words(*load), *load)
        k_accs = accs[q_banks : q_banks + k_banks]
        k_results = [norm_and_rope(acc, 1, "k_result_%d" % b) for b, acc in enumerate(k_accs)]
        v_col = q_cols + k_cols
        for load in (
            [(first, 2, v_col, v_cols) for first in range(4, PASSES - 2, 2)]
            + [(PASSES - 2, 1, v_col, v_cols)]
            + [(PASSES - 1, 1, col, BANK_COLS) for col in range(v_col, COLS, BANK_COLS)]
        ):
            multiply(load_words(*load), *load)

        for out, results in ((out_0, q_results), (out_1, k_results)):
            for b, result in enumerate(results):
                nc.sync.dma_start(
                    out=out[:, b * HEADS_PER_BANK : (b + 1) * HEADS_PER_BANK, :],
                    in_=result[:].rearrange("p h s d -> p h (s d)"),
                )
        for b, acc in enumerate(accs[q_banks + k_banks :]):
            values = work.tile([P, HEADS_PER_BANK, HEAD], F32, name="values")
            flat = values[:].rearrange("p h d -> p (h d)")
            rows = out_2[:, b * HEADS_PER_BANK : (b + 1) * HEADS_PER_BANK, :]
            if b % 2 == 0:
                nc.scalar.copy(out=flat, in_=acc[:])
                nc.scalar.dma_start(out=rows, in_=values[:])
            else:
                nc.vector.tensor_copy(out=flat, in_=acc[:])
                nc.sync.dma_start(out=rows, in_=values[:])
